import numpy as np
import ml_dtypes


def mxq(x, axis, fmt="e4m3"):
    dtype, down = {"e4m3": (ml_dtypes.float8_e4m3fn, 7), "e5m2": (ml_dtypes.float8_e5m2, 14)}[fmt]
    v = np.moveaxis(np.asarray(x, np.float32).astype(ml_dtypes.bfloat16).astype(np.float64), axis, -1)
    blocks = v.reshape(v.shape[:-1] + (-1, 32))
    amax = np.abs(blocks).max(-1, keepdims=True)
    byte = np.maximum(np.where(amax > 0, np.frexp(amax)[1] - 1 + 127, 0) - down, 1)
    scale = np.exp2(byte - 127.0)
    codes = (blocks / scale).astype(np.float32).astype(dtype).astype(np.float64)
    return np.moveaxis((codes * scale).reshape(v.shape), -1, axis)


WIDE = False


def mx_kscale(k):
    if not WIDE:
        return np.ones(k)
    levels = np.array([10, -10, 5, -5, 0])
    a = np.random.permutation(np.resize(levels, k // 512 * 4)).reshape(k // 512, 4)
    idx = np.arange(k)
    return np.exp2(a[idx // 512, idx % 128 // 32])


BF16 = ml_dtypes.bfloat16


def bf(x):
    return np.asarray(x, np.float32).astype(BF16)


def f64(x):
    return np.asarray(x).astype(np.float64)


B, T, DIM, N_HEADS, N_KV_HEADS, HEAD_DIM, QB = 1, 512, 2048, 16, 2, 128, 512
ROPE_THETA = 1000000.0
NQ = N_HEADS * HEAD_DIM
NKV = N_KV_HEADS * HEAD_DIM
HALF = HEAD_DIM // 2


def rotate_half(u):
    return np.concatenate([-u[..., HALF:], u[..., :HALF]], axis=-1)


def rope_tables():
    inv_freq = 1.0 / ROPE_THETA ** (np.arange(0, HEAD_DIM, 2) / HEAD_DIM)
    freqs = np.outer(np.arange(T), inv_freq)
    emb = np.concatenate([freqs, freqs], axis=-1)
    return np.cos(emb), np.sin(emb)


def setup_inputs():
    s = mx_kscale(DIM)
    c, sn = rope_tables()
    w = 1.0 / np.sqrt(DIM)
    return {"x": bf(np.random.standard_normal((B, T, DIM)) * s),
            "cos": bf(c), "sin": bf(sn),
            "wq_k": bf(np.random.standard_normal((DIM, NQ)) * 1.5 * w / s[:, None]),
            "wq_b": bf(np.random.standard_normal(NQ) * 0.3),
            "wk_k": bf(np.random.standard_normal((DIM, NKV)) * 1.5 * w / s[:, None]),
            "wk_b": bf(np.random.standard_normal(NKV) * 0.3),
            "wv_k": bf(np.random.standard_normal((DIM, NKV)) * w / s[:, None]),
            "wv_b": bf(np.random.standard_normal(NKV) * 0.3)}


def reference(x, cos, sin, wq_k, wq_b, wk_k, wk_b, wv_k, wv_b):
    xq = mxq(f64(x), 2, "e4m3")
    q = ((xq @ mxq(f64(wq_k), 0, "e4m3")) + f64(wq_b)).reshape(B, T, N_HEADS, HEAD_DIM)
    k = ((xq @ mxq(f64(wk_k), 0, "e4m3")) + f64(wk_b)).reshape(B, T, N_KV_HEADS, HEAD_DIM)
    v = ((xq @ mxq(f64(wv_k), 0, "e4m3")) + f64(wv_b)).reshape(B, T, N_KV_HEADS, HEAD_DIM)
    c = f64(cos)[None, :, None, :]
    s = f64(sin)[None, :, None, :]
    q = q * c + rotate_half(q) * s
    k = k * c + rotate_half(k) * s
    return q.transpose(0, 2, 1, 3), k.transpose(0, 2, 1, 3), v.transpose(0, 2, 1, 3)

@@ -1,0 +1,256 @@
+from contextlib import ExitStack
+
+import concourse.mybir as mybir
+from concourse.masks import make_identity
+
+F32 = mybir.dt.float32
+BF16 = mybir.dt.bfloat16
+U32 = mybir.dt.uint32
+U8 = mybir.dt.uint8
+FP8X4 = mybir.dt.float8_e4m3fn_x4
+ADD = mybir.AluOpType.add
+MULT = mybir.AluOpType.mult
+IDENTITY = mybir.ActivationFunctionType.Identity
+
+P = 128
+PACK = 4
+K_PASS = P * PACK
+TOKENS = 512
+DIM = 2048
+PASSES = DIM // K_PASS
+TOKENS_PER_PARTITION = TOKENS // P
+HEAD_DIM = 128
+HALF = HEAD_DIM // 2
+Q_HEADS = 16
+K_HEADS = 2
+V_HEADS = 2
+ROTATED_HEADS = Q_HEADS + K_HEADS
+HEADS = ROTATED_HEADS + V_HEADS
+BLOCK_HEADS = 4
+BLOCK_COLS = BLOCK_HEADS * HEAD_DIM
+BLOCKS = HEADS // BLOCK_HEADS
+PAIR = 2
+VECTOR_COLS = 192
+
+FLOPS = 2 * TOKENS * DIM * HEADS * HEAD_DIM
+
+
+def tile_qwencausalselfattention_pa_kernel(
+    tc, x, cos, sin, wq_k, wq_b, wk_k, wk_b, wv_k, wv_b, out_0, out_1, out_2
+):
+    nc = tc.nc
+    with ExitStack() as stack:
+        const = stack.enter_context(tc.tile_pool(name="const", bufs=1))
+        setup = stack.enter_context(tc.tile_pool(name="setup", bufs=1))
+        x_pool = stack.enter_context(tc.tile_pool(name="x_pool", bufs=PASSES))
+        raw_pool = stack.enter_context(tc.tile_pool(name="raw_pool", bufs=BLOCKS * PASSES))
+        grouped_pool = stack.enter_context(tc.tile_pool(name="grouped_pool", bufs=4))
+        codes_pool = stack.enter_context(tc.tile_pool(name="codes_pool", bufs=2))
+        product_pool = stack.enter_context(tc.tile_pool(name="product_pool", bufs=2 * PAIR))
+        result_pool = stack.enter_context(tc.tile_pool(name="result_pool", bufs=3))
+        psum = stack.enter_context(tc.psum_pool(name="psum", bufs=2 * PAIR))
+
+        x_rows = x.flatten_outer_dims().rearrange("(m f) k -> m f k", f=TOKENS_PER_PARTITION)
+        x_raw = []
+        for g in range(PASSES):
+            x_slice = x_pool.tile([P, TOKENS_PER_PARTITION * K_PASS], BF16, name="x_slice")
+            nc.sync.dma_start(
+                out=x_slice[:].rearrange("m (f k) -> m f k", f=TOKENS_PER_PARTITION),
+                in_=x_rows[:, :, g * K_PASS : (g + 1) * K_PASS],
+            )
+            x_raw.append(x_slice)
+
+        cos_raw = setup.tile([P, TOKENS_PER_PARTITION, HEAD_DIM], BF16)
+        sin_raw = setup.tile([P, TOKENS_PER_PARTITION, HEAD_DIM], BF16)
+        nc.scalar.dma_start(
+            out=cos_raw[:], in_=cos.rearrange("(m f) d -> m f d", f=TOKENS_PER_PARTITION)
+        )
+        nc.scalar.dma_start(
+            out=sin_raw[:], in_=sin.rearrange("(m f) d -> m f d", f=TOKENS_PER_PARTITION)
+        )
+        bias_rows = setup.tile([P, HEAD_DIM], BF16)
+        nc.vector.memset(bias_rows[:], 0.0)
+        nc.scalar.dma_start(
+            out=bias_rows[0:Q_HEADS, :], in_=wq_b.rearrange("(h d) -> h d", d=HEAD_DIM)
+        )
+        nc.scalar.dma_start(
+            out=bias_rows[Q_HEADS:ROTATED_HEADS, :], in_=wk_b.rearrange("(h d) -> h d", d=HEAD_DIM)
+        )
+        nc.scalar.dma_start(
+            out=bias_rows[ROTATED_HEADS:HEADS, :], in_=wv_b.rearrange("(h d) -> h d", d=HEAD_DIM)
+        )
+
+        w_raw = []
+        for b in range(BLOCKS):
+            w_raw.append([])
+            for g in range(PASSES):
+                k_rows = slice(g * K_PASS, (g + 1) * K_PASS)
+                raw = raw_pool.tile([P, PACK, BLOCK_COLS], BF16, name="raw")
+                if b * BLOCK_HEADS < Q_HEADS:
+                    nc.sync.dma_start(
+                        out=raw[:],
+                        in_=wq_k[k_rows, b * BLOCK_COLS : (b + 1) * BLOCK_COLS].rearrange(
+                            "(p j) c -> p j c", j=PACK
+                        ),
+                    )
+                else:
+                    k_cols = K_HEADS * HEAD_DIM
+                    nc.sync.dma_start(
+                        out=raw[:, :, 0:k_cols],
+                        in_=wk_k[k_rows, :].rearrange("(p j) c -> p j c", j=PACK),
+                    )
+                    nc.sync.dma_start(
+                        out=raw[:, :, k_cols:BLOCK_COLS],
+                        in_=wv_k[k_rows, :].rearrange("(p j) c -> p j c", j=PACK),
+                    )
+                w_raw[b].append(raw)
+
+        ident = const.tile([P, P], F32)
+        make_identity(nc, ident[:])
+        swap = const.tile([P, P], F32)
+        nc.vector.tensor_copy(out=swap[:, 0:HALF], in_=ident[:, HALF:P])
+        nc.vector.tensor_copy(out=swap[:, HALF:P], in_=ident[:, 0:HALF])
+
+        x_codes = const.tile([P, PASSES, TOKENS], U32, align_bytes=64)
+        x_scales = const.tile([P, PASSES, TOKENS], U8, align_bytes=64)
+        words_per_token = K_PASS // 2
+        half_tokens = TOKENS // 2
+        for g in range(PASSES):
+            x_words = x_raw[g][:].bitcast(F32)
+            x_grouped = x_pool.tile([P, TOKENS * PACK], BF16, align_bytes=64, name="x_grouped")
+            x_grouped_words = x_grouped[:].bitcast(F32)
+            for half in range(2):
+                turned = psum.tile([P, 2 * half_tokens], F32, tag="turned")
+                for u in range(2):
+                    for f in range(2 * half, 2 * half + 2):
+                        column = u * half_tokens + (f - 2 * half) * P
+                        nc.tensor.transpose(
+                            out=turned[:, column : column + P],
+                            in_=x_words[:, f * words_per_token + u : (f + 1) * words_per_token : 2],
+                            identity=ident[:],
+                        )
+                copy = nc.vector.tensor_copy if half == 0 else nc.scalar.copy
+                copy(
+                    out=x_grouped_words[
+                        :, half * 2 * half_tokens : (half + 1) * 2 * half_tokens
+                    ].rearrange("p (n u) -> p n u", u=2),
+                    in_=turned[:].rearrange("p (u n) -> p n u", u=2),
+                )
+            nc.vector.quantize_mx(
+                out=x_codes[:, g, :].bitcast(FP8X4), scales=x_scales[:, g, :], in_=x_grouped[:]
+            )
+
+        cos_f32 = setup.tile([P, TOKENS_PER_PARTITION, HEAD_DIM], F32)
+        sin_f32 = setup.tile([P, TOKENS_PER_PARTITION, HEAD_DIM], F32)
+        nc.vector.tensor_copy(out=cos_f32[:], in_=cos_raw[:])
+        nc.vector.tensor_copy(out=sin_f32[:, :, 0:HALF], in_=sin_raw[:, :, HALF:HEAD_DIM])
+        nc.vector.tensor_scalar_mul(
+            out=sin_f32[:, :, HALF:HEAD_DIM], in0=sin_raw[:, :, 0:HALF], scalar1=-1.0
+        )
+        cos_t = const.tile([P, TOKENS], F32)
+        sin_t = const.tile([P, TOKENS], F32)
+        for table, rows in ((cos_t, cos_f32), (sin_t, sin_f32)):
+            turned = psum.tile([P, TOKENS], F32, tag="turned")
+            for f in range(TOKENS_PER_PARTITION):
+                nc.tensor.transpose(
+                    out=turned[:, f * P : (f + 1) * P], in_=rows[:, f, :], identity=ident[:]
+                )
+            nc.vector.tensor_copy(out=table[:], in_=turned[:])
+
+        bias_f32 = setup.tile([P, HEAD_DIM], F32)
+        nc.vector.tensor_copy(out=bias_f32[:], in_=bias_rows[:])
+        turned = psum.tile([P, TOKENS], F32, tag="turned")
+        nc.tensor.transpose(out=turned[:, 0:P], in_=bias_f32[:], identity=ident[:])
+        bias_t = const.tile([P, HEADS], F32)
+        nc.vector.tensor_copy(out=bias_t[:], in_=turned[:, 0:HEADS])
+
+        result_rows = [
+            out.rearrange("b h (m f) d -> (b h) m (f d)", f=TOKENS_PER_PARTITION)
+            for out in (out_0, out_1, out_2)
+        ]
+
+        def quantise_block(b):
+            w_codes = codes_pool.tile([P, PASSES, BLOCK_COLS], U32, align_bytes=64, name="w_codes")
+            w_scales = codes_pool.tile([P, PASSES, BLOCK_COLS], U8, align_bytes=64, name="w_scales")
+            for g in range(PASSES):
+                grouped = grouped_pool.tile([P, BLOCK_COLS, PACK], BF16, align_bytes=64, name="grouped")
+                for copy, cols in (
+                    (nc.vector.tensor_copy, slice(0, VECTOR_COLS)),
+                    (nc.scalar.copy, slice(VECTOR_COLS, BLOCK_COLS)),
+                ):
+                    copy(
+                        out=grouped[:, cols, :].rearrange("p (c i) j -> p c j i", i=4),
+                        in_=w_raw[b][g][:, :, cols].rearrange("p j (c i) -> p c j i", i=4),
+                    )
+                nc.vector.quantize_mx(
+                    out=w_codes[:, g, :].bitcast(FP8X4),
+                    scales=w_scales[:, g, :],
+                    in_=grouped[:].rearrange("p c j -> p (c j)"),
+                )
+            return w_codes, w_scales
+
+        def project_pair(first_head, w_codes, w_scales):
+            result = result_pool.tile([P, PAIR, TOKENS_PER_PARTITION * HEAD_DIM], F32, name="result")
+            factors = []
+            for h in range(first_head, first_head + PAIR):
+                cols = slice((h % BLOCK_HEADS) * HEAD_DIM, (h % BLOCK_HEADS + 1) * HEAD_DIM)
+                product = psum.tile([P, TOKENS], F32, tag="product")
+                for g in range(PASSES):
+                    nc.tensor.matmul_mx(
+                        out=product[:],
+                        lhsT=w_codes[:, g, cols].bitcast(FP8X4),
+                        lhsT_scale=w_scales[:, g, cols],
+                        rhs=x_codes[:, g, :].bitcast(FP8X4),
+                        rhs_scale=x_scales[:, g, :],
+                        start=(g == 0),
+                        stop=(g == PASSES - 1),
+                    )
+                bias = bias_t[:, h : h + 1]
+                with_cos = product_pool.tile([P, TOKENS], F32, name="with_cos")
+                if h < ROTATED_HEADS:
+                    with_sin = product_pool.tile([P, TOKENS], F32, name="with_sin")
+                    nc.vector.scalar_tensor_tensor(
+                        out=with_cos[:], in0=product[:], scalar=bias, in1=cos_t[:], op0=ADD, op1=MULT
+                    )
+                    nc.vector.scalar_tensor_tensor(
+                        out=with_sin[:], in0=product[:], scalar=bias, in1=sin_t[:], op0=ADD, op1=MULT
+                    )
+                    factors.append((with_cos, with_sin))
+                else:
+                    nc.scalar.activation(
+                        out=with_cos[:], in_=product[:], func=IDENTITY, bias=bias, scale=1.0
+                    )
+                    factors.append((with_cos, None))
+            for i, (with_cos, with_sin) in enumerate(factors):
+                turned = psum.tile([P, TOKENS], F32, tag="turned")
+                for f in range(TOKENS_PER_PARTITION):
+                    cols = slice(f * P, (f + 1) * P)
+                    if with_sin is None:
+                        nc.tensor.transpose(out=turned[:, cols], in_=with_cos[:, cols], identity=ident[:])
+                    else:
+                        nc.tensor.matmul(
+                            out=turned[:, cols], lhsT=with_cos[:, cols], rhs=ident[:],
+                            is_transpose=True, start=True, stop=False,
+                        )
+                        nc.tensor.matmul(
+                            out=turned[:, cols], lhsT=with_sin[:, cols], rhs=swap[:],
+                            is_transpose=True, start=False, stop=True,
+                        )
+                nc.scalar.copy(out=result[:, i, :], in_=turned[:])
+            if first_head < Q_HEADS:
+                rows, first_row = result_rows[0], first_head
+            elif first_head < ROTATED_HEADS:
+                rows, first_row = result_rows[1], first_head - Q_HEADS
+            else:
+                rows, first_row = result_rows[2], first_head - ROTATED_HEADS
+            nc.sync.dma_start(
+                out=rows[first_row : first_row + PAIR].rearrange("h m c -> m h c"), in_=result[:]
+            )
+
+        quantised = quantise_block(0)
+        for b in range(BLOCKS):
+            w_codes, w_scales = quantised
+            if b + 1 < BLOCKS:
+                quantised = quantise_block(b + 1)
+            for first_head in range(b * BLOCK_HEADS, (b + 1) * BLOCK_HEADS, PAIR):
+                project_pair(first_head, w_codes, w_scales)

@@ -10,7 +10,6 @@ U8 = mybir.dt.uint8
 FP8X4 = mybir.dt.float8_e4m3fn_x4
 ADD = mybir.AluOpType.add
 MULT = mybir.AluOpType.mult
-IDENTITY = mybir.ActivationFunctionType.Identity
 
 P = 128
 PACK = 4
@@ -29,8 +28,13 @@ HEADS = ROTATED_HEADS + V_HEADS
 BLOCK_HEADS = 4
 BLOCK_COLS = BLOCK_HEADS * HEAD_DIM
 BLOCKS = HEADS // BLOCK_HEADS
+CHUNKS = BLOCKS * PASSES
 PAIR = 2
-VECTOR_COLS = 192
+PAIRS = HEADS // PAIR
+PAIRS_PER_BLOCK = BLOCK_HEADS // PAIR
+CHUNKS_PER_PAIR = PASSES // PAIRS_PER_BLOCK
+CHUNKS_AHEAD = 2
+VECTOR_COLS = 160
 
 FLOPS = 2 * TOKENS * DIM * HEADS * HEAD_DIM
 
@@ -43,12 +47,13 @@ def tile_qwencausalselfattention_pa_kernel(
         const = stack.enter_context(tc.tile_pool(name="const", bufs=1))
         setup = stack.enter_context(tc.tile_pool(name="setup", bufs=1))
         x_pool = stack.enter_context(tc.tile_pool(name="x_pool", bufs=PASSES))
-        raw_pool = stack.enter_context(tc.tile_pool(name="raw_pool", bufs=BLOCKS * PASSES))
+        raw_pool = stack.enter_context(tc.tile_pool(name="raw_pool", bufs=CHUNKS))
         grouped_pool = stack.enter_context(tc.tile_pool(name="grouped_pool", bufs=4))
-        codes_pool = stack.enter_context(tc.tile_pool(name="codes_pool", bufs=2))
+        codes_pool = stack.enter_context(tc.tile_pool(name="codes_pool", bufs=3))
         product_pool = stack.enter_context(tc.tile_pool(name="product_pool", bufs=2 * PAIR))
         result_pool = stack.enter_context(tc.tile_pool(name="result_pool", bufs=3))
         psum = stack.enter_context(tc.psum_pool(name="psum", bufs=2 * PAIR))
+        stack.enter_context(tc.manual_schedule())
 
         x_rows = x.flatten_outer_dims().rearrange("(m f) k -> m f k", f=TOKENS_PER_PARTITION)
         x_raw = []
@@ -81,29 +86,28 @@ def tile_qwencausalselfattention_pa_kernel(
         )
 
         w_raw = []
-        for b in range(BLOCKS):
-            w_raw.append([])
-            for g in range(PASSES):
-                k_rows = slice(g * K_PASS, (g + 1) * K_PASS)
-                raw = raw_pool.tile([P, PACK, BLOCK_COLS], BF16, name="raw")
-                if b * BLOCK_HEADS < Q_HEADS:
-                    nc.sync.dma_start(
-                        out=raw[:],
-                        in_=wq_k[k_rows, b * BLOCK_COLS : (b + 1) * BLOCK_COLS].rearrange(
-                            "(p j) c -> p j c", j=PACK
-                        ),
-                    )
-                else:
-                    k_cols = K_HEADS * HEAD_DIM
-                    nc.sync.dma_start(
-                        out=raw[:, :, 0:k_cols],
-                        in_=wk_k[k_rows, :].rearrange("(p j) c -> p j c", j=PACK),
-                    )
-                    nc.sync.dma_start(
-                        out=raw[:, :, k_cols:BLOCK_COLS],
-                        in_=wv_k[k_rows, :].rearrange("(p j) c -> p j c", j=PACK),
-                    )
-                w_raw[b].append(raw)
+        for n in range(CHUNKS):
+            b, g = divmod(n, PASSES)
+            k_rows = slice(g * K_PASS, (g + 1) * K_PASS)
+            raw = raw_pool.tile([P, PACK, BLOCK_COLS], BF16, name="raw")
+            if b * BLOCK_HEADS < Q_HEADS:
+                nc.sync.dma_start(
+                    out=raw[:],
+                    in_=wq_k[k_rows, b * BLOCK_COLS : (b + 1) * BLOCK_COLS].rearrange(
+                        "(p j) c -> p j c", j=PACK
+                    ),
+                )
+            else:
+                k_cols = K_HEADS * HEAD_DIM
+                nc.sync.dma_start(
+                    out=raw[:, :, 0:k_cols],
+                    in_=wk_k[k_rows, :].rearrange("(p j) c -> p j c", j=PACK),
+                )
+                nc.sync.dma_start(
+                    out=raw[:, :, k_cols:BLOCK_COLS],
+                    in_=wv_k[k_rows, :].rearrange("(p j) c -> p j c", j=PACK),
+                )
+            w_raw.append(raw)
 
         ident = const.tile([P, P], F32)
         make_identity(nc, ident[:])
@@ -115,30 +119,37 @@ def tile_qwencausalselfattention_pa_kernel(
         x_scales = const.tile([P, PASSES, TOKENS], U8, align_bytes=64)
         words_per_token = K_PASS // 2
         half_tokens = TOKENS // 2
-        for g in range(PASSES):
-            x_words = x_raw[g][:].bitcast(F32)
-            x_grouped = x_pool.tile([P, TOKENS * PACK], BF16, align_bytes=64, name="x_grouped")
-            x_grouped_words = x_grouped[:].bitcast(F32)
-            for half in range(2):
-                turned = psum.tile([P, 2 * half_tokens], F32, tag="turned")
-                for u in range(2):
-                    for f in range(2 * half, 2 * half + 2):
-                        column = u * half_tokens + (f - 2 * half) * P
-                        nc.tensor.transpose(
-                            out=turned[:, column : column + P],
-                            in_=x_words[:, f * words_per_token + u : (f + 1) * words_per_token : 2],
-                            identity=ident[:],
-                        )
-                copy = nc.vector.tensor_copy if half == 0 else nc.scalar.copy
-                copy(
-                    out=x_grouped_words[
-                        :, half * 2 * half_tokens : (half + 1) * 2 * half_tokens
-                    ].rearrange("p (n u) -> p n u", u=2),
-                    in_=turned[:].rearrange("p (u n) -> p n u", u=2),
+        x_grouped = []
+        for g in range(PASSES + 1):
+            if g < PASSES:
+                x_words = x_raw[g][:].bitcast(F32)
+                grouped = x_pool.tile([P, TOKENS * PACK], BF16, align_bytes=64, name="x_grouped")
+                x_grouped.append(grouped)
+                for half in range(2):
+                    turned = psum.tile([P, TOKENS], F32, tag="turned")
+                    for u in range(2):
+                        for f in range(2 * half, 2 * half + 2):
+                            column = u * half_tokens + (f - 2 * half) * P
+                            nc.tensor.transpose(
+                                out=turned[:, column : column + P],
+                                in_=x_words[
+                                    :, f * words_per_token + u : (f + 1) * words_per_token : 2
+                                ],
+                                identity=ident[:],
+                            )
+                    copy = nc.vector.tensor_copy if half == 0 else nc.scalar.copy
+                    copy(
+                        out=grouped[:]
+                        .bitcast(F32)[:, half * TOKENS : (half + 1) * TOKENS]
+                        .rearrange("p (n u) -> p n u", u=2),
+                        in_=turned[:].rearrange("p (u n) -> p n u", u=2),
+                    )
+            if g > 0:
+                nc.vector.quantize_mx(
+                    out=x_codes[:, g - 1, :].bitcast(FP8X4),
+                    scales=x_scales[:, g - 1, :],
+                    in_=x_grouped[g - 1][:],
                 )
-            nc.vector.quantize_mx(
-                out=x_codes[:, g, :].bitcast(FP8X4), scales=x_scales[:, g, :], in_=x_grouped[:]
-            )
 
         cos_f32 = setup.tile([P, TOKENS_PER_PARTITION, HEAD_DIM], F32)
         sin_f32 = setup.tile([P, TOKENS_PER_PARTITION, HEAD_DIM], F32)
@@ -147,6 +158,8 @@ def tile_qwencausalselfattention_pa_kernel(
         nc.vector.tensor_scalar_mul(
             out=sin_f32[:, :, HALF:HEAD_DIM], in0=sin_raw[:, :, 0:HALF], scalar1=-1.0
         )
+        bias_f32 = setup.tile([P, HEAD_DIM], F32)
+        nc.vector.tensor_copy(out=bias_f32[:], in_=bias_rows[:])
         cos_t = const.tile([P, TOKENS], F32)
         sin_t = const.tile([P, TOKENS], F32)
         for table, rows in ((cos_t, cos_f32), (sin_t, sin_f32)):
@@ -156,9 +169,6 @@ def tile_qwencausalselfattention_pa_kernel(
                     out=turned[:, f * P : (f + 1) * P], in_=rows[:, f, :], identity=ident[:]
                 )
             nc.vector.tensor_copy(out=table[:], in_=turned[:])
-
-        bias_f32 = setup.tile([P, HEAD_DIM], F32)
-        nc.vector.tensor_copy(out=bias_f32[:], in_=bias_rows[:])
         turned = psum.tile([P, TOKENS], F32, tag="turned")
         nc.tensor.transpose(out=turned[:, 0:P], in_=bias_f32[:], identity=ident[:])
         bias_t = const.tile([P, HEADS], F32)
@@ -169,64 +179,92 @@ def tile_qwencausalselfattention_pa_kernel(
             for out in (out_0, out_1, out_2)
         ]
 
-        def quantise_block(b):
-            w_codes = codes_pool.tile([P, PASSES, BLOCK_COLS], U32, align_bytes=64, name="w_codes")
-            w_scales = codes_pool.tile([P, PASSES, BLOCK_COLS], U8, align_bytes=64, name="w_scales")
-            for g in range(PASSES):
-                grouped = grouped_pool.tile([P, BLOCK_COLS, PACK], BF16, align_bytes=64, name="grouped")
-                for copy, cols in (
-                    (nc.vector.tensor_copy, slice(0, VECTOR_COLS)),
-                    (nc.scalar.copy, slice(VECTOR_COLS, BLOCK_COLS)),
-                ):
-                    copy(
-                        out=grouped[:, cols, :].rearrange("p (c i) j -> p c j i", i=4),
-                        in_=w_raw[b][g][:, :, cols].rearrange("p j (c i) -> p c j i", i=4),
-                    )
-                nc.vector.quantize_mx(
-                    out=w_codes[:, g, :].bitcast(FP8X4),
-                    scales=w_scales[:, g, :],
-                    in_=grouped[:].rearrange("p c j -> p (c j)"),
-                )
-            return w_codes, w_scales
+        w_grouped = {}
+        w_codes = {}
+        w_scales = {}
+        products = {}
+        factors = {}
+        results = {}
 
-        def project_pair(first_head, w_codes, w_scales):
-            result = result_pool.tile([P, PAIR, TOKENS_PER_PARTITION * HEAD_DIM], F32, name="result")
-            factors = []
-            for h in range(first_head, first_head + PAIR):
-                cols = slice((h % BLOCK_HEADS) * HEAD_DIM, (h % BLOCK_HEADS + 1) * HEAD_DIM)
-                product = psum.tile([P, TOKENS], F32, tag="product")
+        def regroup(n):
+            grouped = grouped_pool.tile([P, BLOCK_COLS, PACK], BF16, align_bytes=64, name="grouped")
+            w_grouped[n] = grouped
+            for copy, cols in (
+                (nc.vector.tensor_copy, slice(0, VECTOR_COLS)),
+                (nc.scalar.copy, slice(VECTOR_COLS, BLOCK_COLS)),
+            ):
+                copy(
+                    out=grouped[:, cols, :].rearrange("p (c i) j -> p c j i", i=4),
+                    in_=w_raw[n][:, :, cols].rearrange("p j (c i) -> p c j i", i=4),
+                )
+
+        def quantise(n):
+            b, g = divmod(n, PASSES)
+            if g == 0:
+                w_codes[b] = codes_pool.tile(
+                    [P, PASSES, BLOCK_COLS], U32, align_bytes=64, name="w_codes"
+                )
+                w_scales[b] = codes_pool.tile(
+                    [P, PASSES, BLOCK_COLS], U8, align_bytes=64, name="w_scales"
+                )
+            nc.vector.quantize_mx(
+                out=w_codes[b][:, g, :].bitcast(FP8X4),
+                scales=w_scales[b][:, g, :],
+                in_=w_grouped[n][:].rearrange("p c j -> p (c j)"),
+            )
+
+        def multiply(h, g):
+            if g == 0:
+                products[h] = psum.tile([P, TOKENS], F32, tag="product", name="product")
+            b, i = divmod(h, BLOCK_HEADS)
+            cols = slice(i * HEAD_DIM, (i + 1) * HEAD_DIM)
+            nc.tensor.matmul_mx(
+                out=products[h][:],
+                lhsT=w_codes[b][:, g, cols].bitcast(FP8X4),
+                lhsT_scale=w_scales[b][:, g, cols],
+                rhs=x_codes[:, g, :].bitcast(FP8X4),
+                rhs_scale=x_scales[:, g, :],
+                start=(g == 0),
+                stop=(g == PASSES - 1),
+            )
+
+        def heads_of(pair):
+            return range(pair * PAIR, (pair + 1) * PAIR)
+
+        def multiply_pair(pair):
+            for h in heads_of(pair):
                 for g in range(PASSES):
-                    nc.tensor.matmul_mx(
-                        out=product[:],
-                        lhsT=w_codes[:, g, cols].bitcast(FP8X4),
-                        lhsT_scale=w_scales[:, g, cols],
-                        rhs=x_codes[:, g, :].bitcast(FP8X4),
-                        rhs_scale=x_scales[:, g, :],
-                        start=(g == 0),
-                        stop=(g == PASSES - 1),
-                    )
+                    multiply(h, g)
+
+        def add_bias_and_scale(pair):
+            for h in heads_of(pair):
                 bias = bias_t[:, h : h + 1]
                 with_cos = product_pool.tile([P, TOKENS], F32, name="with_cos")
                 if h < ROTATED_HEADS:
                     with_sin = product_pool.tile([P, TOKENS], F32, name="with_sin")
                     nc.vector.scalar_tensor_tensor(
-                        out=with_cos[:], in0=product[:], scalar=bias, in1=cos_t[:], op0=ADD, op1=MULT
+                        out=with_cos[:], in0=products[h][:], scalar=bias, in1=cos_t[:], op0=ADD, op1=MULT
                     )
                     nc.vector.scalar_tensor_tensor(
-                        out=with_sin[:], in0=product[:], scalar=bias, in1=sin_t[:], op0=ADD, op1=MULT
+                        out=with_sin[:], in0=products[h][:], scalar=bias, in1=sin_t[:], op0=ADD, op1=MULT
                     )
-                    factors.append((with_cos, with_sin))
+                    factors[h] = (with_cos, with_sin)
                 else:
-                    nc.scalar.activation(
-                        out=with_cos[:], in_=product[:], func=IDENTITY, bias=bias, scale=1.0
-                    )
-                    factors.append((with_cos, None))
-            for i, (with_cos, with_sin) in enumerate(factors):
-                turned = psum.tile([P, TOKENS], F32, tag="turned")
+                    nc.vector.tensor_scalar_add(out=with_cos[:], in0=products[h][:], scalar1=bias)
+                    factors[h] = (with_cos, None)
+
+        def turn_back(pair):
+            turned_banks = []
+            for h in heads_of(pair):
+                with_cos, with_sin = factors[h]
+                turned = psum.tile([P, TOKENS], F32, tag="turned", name="turned")
+                turned_banks.append(turned)
                 for f in range(TOKENS_PER_PARTITION):
                     cols = slice(f * P, (f + 1) * P)
                     if with_sin is None:
-                        nc.tensor.transpose(out=turned[:, cols], in_=with_cos[:, cols], identity=ident[:])
+                        nc.tensor.transpose(
+                            out=turned[:, cols], in_=with_cos[:, cols], identity=ident[:]
+                        )
                     else:
                         nc.tensor.matmul(
                             out=turned[:, cols], lhsT=with_cos[:, cols], rhs=ident[:],
@@ -236,21 +274,52 @@ def tile_qwencausalselfattention_pa_kernel(
                             out=turned[:, cols], lhsT=with_sin[:, cols], rhs=swap[:],
                             is_transpose=True, start=False, stop=True,
                         )
+            return turned_banks
+
+        def copy_out(pair, turned_banks):
+            result = result_pool.tile([P, PAIR, TOKENS_PER_PARTITION * HEAD_DIM], F32, name="result")
+            results[pair] = result
+            for i, turned in enumerate(turned_banks):
                 nc.scalar.copy(out=result[:, i, :], in_=turned[:])
+
+        def store(pair):
+            first_head = pair * PAIR
             if first_head < Q_HEADS:
                 rows, first_row = result_rows[0], first_head
             elif first_head < ROTATED_HEADS:
                 rows, first_row = result_rows[1], first_head - Q_HEADS
             else:
                 rows, first_row = result_rows[2], first_head - ROTATED_HEADS
-            nc.sync.dma_start(
-                out=rows[first_row : first_row + PAIR].rearrange("h m c -> m h c"), in_=result[:]
+            nc.scalar.dma_start(
+                out=rows[first_row : first_row + PAIR].rearrange("h m c -> m h c"),
+                in_=results[pair][:],
             )
 
-        quantised = quantise_block(0)
-        for b in range(BLOCKS):
-            w_codes, w_scales = quantised
-            if b + 1 < BLOCKS:
-                quantised = quantise_block(b + 1)
-            for first_head in range(b * BLOCK_HEADS, (b + 1) * BLOCK_HEADS, PAIR):
-                project_pair(first_head, w_codes, w_scales)
+        first_chunks = PASSES + CHUNKS_AHEAD
+        for n in range(first_chunks + 1):
+            if n < first_chunks:
+                regroup(n)
+            if n > 0:
+                quantise(n - 1)
+                if n - 1 < PASSES:
+                    for h in range(BLOCK_HEADS):
+                        multiply(h, n - 1)
+
+        next_chunk = first_chunks
+        for pair in range(PAIRS):
+            if PAIRS_PER_BLOCK <= pair + 1 < PAIRS:
+                multiply_pair(pair + 1)
+            add_bias_and_scale(pair)
+            turned_banks = turn_back(pair)
+            chunks = range(next_chunk, min(next_chunk + CHUNKS_PER_PAIR, CHUNKS))
+            next_chunk += CHUNKS_PER_PAIR
+            for n in chunks:
+                regroup(n)
+                if n == chunks[0] and pair > 0:
+                    store(pair - 1)
+            for n in chunks:
+                quantise(n)
+            if len(chunks) == 0 and pair > 0:
+                store(pair - 1)
+            copy_out(pair, turned_banks)
+        store(PAIRS - 1)

@@ -34,7 +34,7 @@ PAIRS = HEADS // PAIR
 PAIRS_PER_BLOCK = BLOCK_HEADS // PAIR
 CHUNKS_PER_PAIR = PASSES // PAIRS_PER_BLOCK
 CHUNKS_AHEAD = 2
-VECTOR_COLS = 160
+VECTOR_COLS = 64
 
 FLOPS = 2 * TOKENS * DIM * HEADS * HEAD_DIM
 

@@ -29,12 +29,12 @@ BLOCK_HEADS = 4
 BLOCK_COLS = BLOCK_HEADS * HEAD_DIM
 BLOCKS = HEADS // BLOCK_HEADS
 CHUNKS = BLOCKS * PASSES
+CHUNKS_PER_HEAD = PASSES // BLOCK_HEADS
 PAIR = 2
-PAIRS = HEADS // PAIR
-PAIRS_PER_BLOCK = BLOCK_HEADS // PAIR
-CHUNKS_PER_PAIR = PASSES // PAIRS_PER_BLOCK
-CHUNKS_AHEAD = 2
-VECTOR_COLS = 64
+RUN = 1
+FIRST_CHUNKS = PASSES + 2
+PSUM_BANKS_PER_KIND = 4
+VECTOR_COLS = 160
 
 FLOPS = 2 * TOKENS * DIM * HEADS * HEAD_DIM
 
@@ -50,9 +50,9 @@ def tile_qwencausalselfattention_pa_kernel(
         raw_pool = stack.enter_context(tc.tile_pool(name="raw_pool", bufs=CHUNKS))
         grouped_pool = stack.enter_context(tc.tile_pool(name="grouped_pool", bufs=4))
         codes_pool = stack.enter_context(tc.tile_pool(name="codes_pool", bufs=3))
-        product_pool = stack.enter_context(tc.tile_pool(name="product_pool", bufs=2 * PAIR))
+        product_pool = stack.enter_context(tc.tile_pool(name="product_pool", bufs=4))
         result_pool = stack.enter_context(tc.tile_pool(name="result_pool", bufs=3))
-        psum = stack.enter_context(tc.psum_pool(name="psum", bufs=2 * PAIR))
+        psum = stack.enter_context(tc.psum_pool(name="psum", bufs=PSUM_BANKS_PER_KIND))
         stack.enter_context(tc.manual_schedule())
 
         x_rows = x.flatten_outer_dims().rearrange("(m f) k -> m f k", f=TOKENS_PER_PARTITION)
@@ -184,6 +184,7 @@ def tile_qwencausalselfattention_pa_kernel(
         w_scales = {}
         products = {}
         factors = {}
+        turned_banks = {}
         results = {}
 
         def regroup(n):
@@ -228,59 +229,47 @@ def tile_qwencausalselfattention_pa_kernel(
                 stop=(g == PASSES - 1),
             )
 
-        def heads_of(pair):
-            return range(pair * PAIR, (pair + 1) * PAIR)
+        def add_bias_and_scale(h):
+            bias = bias_t[:, h : h + 1]
+            with_cos = product_pool.tile([P, TOKENS], F32, name="with_cos")
+            if h < ROTATED_HEADS:
+                with_sin = product_pool.tile([P, TOKENS], F32, name="with_sin")
+                nc.vector.scalar_tensor_tensor(
+                    out=with_cos[:], in0=products[h][:], scalar=bias, in1=cos_t[:], op0=ADD, op1=MULT
+                )
+                nc.vector.scalar_tensor_tensor(
+                    out=with_sin[:], in0=products[h][:], scalar=bias, in1=sin_t[:], op0=ADD, op1=MULT
+                )
+                factors[h] = (with_cos, with_sin)
+            else:
+                nc.vector.tensor_scalar_add(out=with_cos[:], in0=products[h][:], scalar1=bias)
+                factors[h] = (with_cos, None)
 
-        def multiply_pair(pair):
-            for h in heads_of(pair):
-                for g in range(PASSES):
-                    multiply(h, g)
-
-        def add_bias_and_scale(pair):
-            for h in heads_of(pair):
-                bias = bias_t[:, h : h + 1]
-                with_cos = product_pool.tile([P, TOKENS], F32, name="with_cos")
-                if h < ROTATED_HEADS:
-                    with_sin = product_pool.tile([P, TOKENS], F32, name="with_sin")
-                    nc.vector.scalar_tensor_tensor(
-                        out=with_cos[:], in0=products[h][:], scalar=bias, in1=cos_t[:], op0=ADD, op1=MULT
-                    )
-                    nc.vector.scalar_tensor_tensor(
-                        out=with_sin[:], in0=products[h][:], scalar=bias, in1=sin_t[:], op0=ADD, op1=MULT
-                    )
-                    factors[h] = (with_cos, with_sin)
+        def turn_back(h):
+            with_cos, with_sin = factors[h]
+            turned = psum.tile([P, TOKENS], F32, tag="turned", name="turned")
+            turned_banks[h] = turned
+            for f in range(TOKENS_PER_PARTITION):
+                cols = slice(f * P, (f + 1) * P)
+                if with_sin is None:
+                    nc.tensor.transpose(out=turned[:, cols], in_=with_cos[:, cols], identity=ident[:])
                 else:
-                    nc.vector.tensor_scalar_add(out=with_cos[:], in0=products[h][:], scalar1=bias)
-                    factors[h] = (with_cos, None)
+                    nc.tensor.matmul(
+                        out=turned[:, cols], lhsT=with_cos[:, cols], rhs=ident[:],
+                        is_transpose=True, start=True, stop=False,
+                    )
+                    nc.tensor.matmul(
+                        out=turned[:, cols], lhsT=with_sin[:, cols], rhs=swap[:],
+                        is_transpose=True, start=False, stop=True,
+                    )
 
-        def turn_back(pair):
-            turned_banks = []
-            for h in heads_of(pair):
-                with_cos, with_sin = factors[h]
-                turned = psum.tile([P, TOKENS], F32, tag="turned", name="turned")
-                turned_banks.append(turned)
-                for f in range(TOKENS_PER_PARTITION):
-                    cols = slice(f * P, (f + 1) * P)
-                    if with_sin is None:
-                        nc.tensor.transpose(
-                            out=turned[:, cols], in_=with_cos[:, cols], identity=ident[:]
-                        )
-                    else:
-                        nc.tensor.matmul(
-                            out=turned[:, cols], lhsT=with_cos[:, cols], rhs=ident[:],
-                            is_transpose=True, start=True, stop=False,
-                        )
-                        nc.tensor.matmul(
-                            out=turned[:, cols], lhsT=with_sin[:, cols], rhs=swap[:],
-                            is_transpose=True, start=False, stop=True,
-                        )
-            return turned_banks
-
-        def copy_out(pair, turned_banks):
-            result = result_pool.tile([P, PAIR, TOKENS_PER_PARTITION * HEAD_DIM], F32, name="result")
-            results[pair] = result
-            for i, turned in enumerate(turned_banks):
-                nc.scalar.copy(out=result[:, i, :], in_=turned[:])
+        def copy_out(h):
+            pair, i = divmod(h, PAIR)
+            if i == 0:
+                results[pair] = result_pool.tile(
+                    [P, PAIR, TOKENS_PER_PARTITION * HEAD_DIM], F32, name="result"
+                )
+            nc.scalar.copy(out=results[pair][:, i, :], in_=turned_banks[h][:])
 
         def store(pair):
             first_head = pair * PAIR
@@ -295,31 +284,34 @@ def tile_qwencausalselfattention_pa_kernel(
                 in_=results[pair][:],
             )
 
-        first_chunks = PASSES + CHUNKS_AHEAD
-        for n in range(first_chunks + 1):
-            if n < first_chunks:
+        def prepare(n):
+            if n < CHUNKS:
                 regroup(n)
-            if n > 0:
+            if 0 < n <= CHUNKS:
                 quantise(n - 1)
-                if n - 1 < PASSES:
-                    for h in range(BLOCK_HEADS):
-                        multiply(h, n - 1)
 
-        next_chunk = first_chunks
-        for pair in range(PAIRS):
-            if PAIRS_PER_BLOCK <= pair + 1 < PAIRS:
-                multiply_pair(pair + 1)
-            add_bias_and_scale(pair)
-            turned_banks = turn_back(pair)
-            chunks = range(next_chunk, min(next_chunk + CHUNKS_PER_PAIR, CHUNKS))
-            next_chunk += CHUNKS_PER_PAIR
-            for n in chunks:
-                regroup(n)
-                if n == chunks[0] and pair > 0:
-                    store(pair - 1)
-            for n in chunks:
-                quantise(n)
-            if len(chunks) == 0 and pair > 0:
-                store(pair - 1)
-            copy_out(pair, turned_banks)
-        store(PAIRS - 1)
+        for n in range(FIRST_CHUNKS):
+            prepare(n)
+            if 0 < n <= PASSES:
+                for h in range(BLOCK_HEADS):
+                    multiply(h, n - 1)
+
+        next_chunk = FIRST_CHUNKS
+        for first_head in range(0, HEADS, RUN):
+            heads = range(first_head, first_head + RUN)
+            for h in heads:
+                if BLOCK_HEADS <= h + RUN < HEADS:
+                    for g in range(PASSES):
+                        multiply(h + RUN, g)
+            for h in heads:
+                add_bias_and_scale(h)
+            for h in heads:
+                turn_back(h)
+            for n in range(next_chunk, next_chunk + RUN * CHUNKS_PER_HEAD):
+                prepare(n)
+                if n == next_chunk and first_head > 0 and first_head % PAIR == 0:
+                    store(first_head // PAIR - 1)
+            next_chunk += RUN * CHUNKS_PER_HEAD
+            for h in heads:
+                copy_out(h)
+        store(HEADS // PAIR - 1)

@@ -10,6 +10,7 @@ U8 = mybir.dt.uint8
 FP8X4 = mybir.dt.float8_e4m3fn_x4
 ADD = mybir.AluOpType.add
 MULT = mybir.AluOpType.mult
+IDENTITY = mybir.ActivationFunctionType.Identity
 
 P = 128
 PACK = 4
@@ -21,20 +22,21 @@ TOKENS_PER_PARTITION = TOKENS // P
 HEAD_DIM = 128
 HALF = HEAD_DIM // 2
 Q_HEADS = 16
-K_HEADS = 2
 V_HEADS = 2
-ROTATED_HEADS = Q_HEADS + K_HEADS
-HEADS = ROTATED_HEADS + V_HEADS
+K_HEADS = 2
+FIRST_K_HEAD = Q_HEADS + V_HEADS
+HEADS = FIRST_K_HEAD + K_HEADS
 BLOCK_HEADS = 4
 BLOCK_COLS = BLOCK_HEADS * HEAD_DIM
 BLOCKS = HEADS // BLOCK_HEADS
 CHUNKS = BLOCKS * PASSES
 CHUNKS_PER_HEAD = PASSES // BLOCK_HEADS
 PAIR = 2
-RUN = 1
-FIRST_CHUNKS = PASSES + 2
+RUN = 2
+FIRST_CHUNKS = PASSES + 3
 PSUM_BANKS_PER_KIND = 4
-VECTOR_COLS = 160
+VECTOR_COLS_FIRST = 256
+VECTOR_COLS = 128
 
 FLOPS = 2 * TOKENS * DIM * HEADS * HEAD_DIM
 
@@ -79,10 +81,10 @@ def tile_qwencausalselfattention_pa_kernel(
             out=bias_rows[0:Q_HEADS, :], in_=wq_b.rearrange("(h d) -> h d", d=HEAD_DIM)
         )
         nc.scalar.dma_start(
-            out=bias_rows[Q_HEADS:ROTATED_HEADS, :], in_=wk_b.rearrange("(h d) -> h d", d=HEAD_DIM)
+            out=bias_rows[Q_HEADS:FIRST_K_HEAD, :], in_=wv_b.rearrange("(h d) -> h d", d=HEAD_DIM)
         )
         nc.scalar.dma_start(
-            out=bias_rows[ROTATED_HEADS:HEADS, :], in_=wv_b.rearrange("(h d) -> h d", d=HEAD_DIM)
+            out=bias_rows[FIRST_K_HEAD:HEADS, :], in_=wk_b.rearrange("(h d) -> h d", d=HEAD_DIM)
         )
 
         w_raw = []
@@ -98,14 +100,14 @@ def tile_qwencausalselfattention_pa_kernel(
                     ),
                 )
             else:
-                k_cols = K_HEADS * HEAD_DIM
+                v_cols = V_HEADS * HEAD_DIM
                 nc.sync.dma_start(
-                    out=raw[:, :, 0:k_cols],
-                    in_=wk_k[k_rows, :].rearrange("(p j) c -> p j c", j=PACK),
+                    out=raw[:, :, 0:v_cols],
+                    in_=wv_k[k_rows, :].rearrange("(p j) c -> p j c", j=PACK),
                 )
                 nc.sync.dma_start(
-                    out=raw[:, :, k_cols:BLOCK_COLS],
-                    in_=wv_k[k_rows, :].rearrange("(p j) c -> p j c", j=PACK),
+                    out=raw[:, :, v_cols:BLOCK_COLS],
+                    in_=wk_k[k_rows, :].rearrange("(p j) c -> p j c", j=PACK),
                 )
             w_raw.append(raw)
 
@@ -114,6 +116,28 @@ def tile_qwencausalselfattention_pa_kernel(
         swap = const.tile([P, P], F32)
         nc.vector.tensor_copy(out=swap[:, 0:HALF], in_=ident[:, HALF:P])
         nc.vector.tensor_copy(out=swap[:, HALF:P], in_=ident[:, 0:HALF])
+
+        cos_f32 = setup.tile([P, TOKENS_PER_PARTITION, HEAD_DIM], F32)
+        sin_f32 = setup.tile([P, TOKENS_PER_PARTITION, HEAD_DIM], F32)
+        nc.vector.tensor_copy(out=cos_f32[:], in_=cos_raw[:])
+        nc.vector.tensor_copy(out=sin_f32[:, :, 0:HALF], in_=sin_raw[:, :, HALF:HEAD_DIM])
+        nc.vector.tensor_scalar_mul(
+            out=sin_f32[:, :, HALF:HEAD_DIM], in0=sin_raw[:, :, 0:HALF], scalar1=-1.0
+        )
+        bias_f32 = setup.tile([P, HEAD_DIM], F32)
+        nc.vector.tensor_copy(out=bias_f32[:], in_=bias_rows[:])
+        tables = const.tile([P, 2, TOKENS], F32)
+        for i, rows in enumerate((cos_f32, sin_f32)):
+            turned = psum.tile([P, TOKENS], F32, tag="turned")
+            for f in range(TOKENS_PER_PARTITION):
+                nc.tensor.transpose(
+                    out=turned[:, f * P : (f + 1) * P], in_=rows[:, f, :], identity=ident[:]
+                )
+            nc.scalar.copy(out=tables[:, i, :], in_=turned[:])
+        turned = psum.tile([P, TOKENS], F32, tag="turned")
+        nc.tensor.transpose(out=turned[:, 0:P], in_=bias_f32[:], identity=ident[:])
+        bias_t = const.tile([P, HEADS], F32)
+        nc.scalar.copy(out=bias_t[:], in_=turned[:, 0:HEADS])
 
         x_codes = const.tile([P, PASSES, TOKENS], U32, align_bytes=64)
         x_scales = const.tile([P, PASSES, TOKENS], U8, align_bytes=64)
@@ -151,29 +175,6 @@ def tile_qwencausalselfattention_pa_kernel(
                     in_=x_grouped[g - 1][:],
                 )
 
-        cos_f32 = setup.tile([P, TOKENS_PER_PARTITION, HEAD_DIM], F32)
-        sin_f32 = setup.tile([P, TOKENS_PER_PARTITION, HEAD_DIM], F32)
-        nc.vector.tensor_copy(out=cos_f32[:], in_=cos_raw[:])
-        nc.vector.tensor_copy(out=sin_f32[:, :, 0:HALF], in_=sin_raw[:, :, HALF:HEAD_DIM])
-        nc.vector.tensor_scalar_mul(
-            out=sin_f32[:, :, HALF:HEAD_DIM], in0=sin_raw[:, :, 0:HALF], scalar1=-1.0
-        )
-        bias_f32 = setup.tile([P, HEAD_DIM], F32)
-        nc.vector.tensor_copy(out=bias_f32[:], in_=bias_rows[:])
-        cos_t = const.tile([P, TOKENS], F32)
-        sin_t = const.tile([P, TOKENS], F32)
-        for table, rows in ((cos_t, cos_f32), (sin_t, sin_f32)):
-            turned = psum.tile([P, TOKENS], F32, tag="turned")
-            for f in range(TOKENS_PER_PARTITION):
-                nc.tensor.transpose(
-                    out=turned[:, f * P : (f + 1) * P], in_=rows[:, f, :], identity=ident[:]
-                )
-            nc.vector.tensor_copy(out=table[:], in_=turned[:])
-        turned = psum.tile([P, TOKENS], F32, tag="turned")
-        nc.tensor.transpose(out=turned[:, 0:P], in_=bias_f32[:], identity=ident[:])
-        bias_t = const.tile([P, HEADS], F32)
-        nc.vector.tensor_copy(out=bias_t[:], in_=turned[:, 0:HEADS])
-
         result_rows = [
             out.rearrange("b h (m f) d -> (b h) m (f d)", f=TOKENS_PER_PARTITION)
             for out in (out_0, out_1, out_2)
@@ -187,12 +188,16 @@ def tile_qwencausalselfattention_pa_kernel(
         turned_banks = {}
         results = {}
 
+        def rotated(h):
+            return h < Q_HEADS or h >= FIRST_K_HEAD
+
         def regroup(n):
             grouped = grouped_pool.tile([P, BLOCK_COLS, PACK], BF16, align_bytes=64, name="grouped")
             w_grouped[n] = grouped
+            vector_cols = VECTOR_COLS_FIRST if n < FIRST_CHUNKS else VECTOR_COLS
             for copy, cols in (
-                (nc.vector.tensor_copy, slice(0, VECTOR_COLS)),
-                (nc.scalar.copy, slice(VECTOR_COLS, BLOCK_COLS)),
+                (nc.vector.tensor_copy, slice(0, vector_cols)),
+                (nc.scalar.copy, slice(vector_cols, BLOCK_COLS)),
             ):
                 copy(
                     out=grouped[:, cols, :].rearrange("p (c i) j -> p c j i", i=4),
@@ -231,37 +236,39 @@ def tile_qwencausalselfattention_pa_kernel(
 
         def add_bias_and_scale(h):
             bias = bias_t[:, h : h + 1]
-            with_cos = product_pool.tile([P, TOKENS], F32, name="with_cos")
-            if h < ROTATED_HEADS:
-                with_sin = product_pool.tile([P, TOKENS], F32, name="with_sin")
+            both = product_pool.tile([P, 2, TOKENS], F32, name="both")
+            factors[h] = both
+            if rotated(h):
                 nc.vector.scalar_tensor_tensor(
-                    out=with_cos[:], in0=products[h][:], scalar=bias, in1=cos_t[:], op0=ADD, op1=MULT
+                    out=both[:],
+                    in0=products[h][:].unsqueeze(1).to_broadcast([P, 2, TOKENS]),
+                    scalar=bias,
+                    in1=tables[:],
+                    op0=ADD,
+                    op1=MULT,
                 )
-                nc.vector.scalar_tensor_tensor(
-                    out=with_sin[:], in0=products[h][:], scalar=bias, in1=sin_t[:], op0=ADD, op1=MULT
-                )
-                factors[h] = (with_cos, with_sin)
             else:
-                nc.vector.tensor_scalar_add(out=with_cos[:], in0=products[h][:], scalar1=bias)
-                factors[h] = (with_cos, None)
+                nc.scalar.activation(
+                    out=both[:, 0, :], in_=products[h][:], func=IDENTITY, bias=bias, scale=1.0
+                )
 
         def turn_back(h):
-            with_cos, with_sin = factors[h]
+            both = factors[h]
             turned = psum.tile([P, TOKENS], F32, tag="turned", name="turned")
             turned_banks[h] = turned
             for f in range(TOKENS_PER_PARTITION):
                 cols = slice(f * P, (f + 1) * P)
-                if with_sin is None:
-                    nc.tensor.transpose(out=turned[:, cols], in_=with_cos[:, cols], identity=ident[:])
-                else:
+                if rotated(h):
                     nc.tensor.matmul(
-                        out=turned[:, cols], lhsT=with_cos[:, cols], rhs=ident[:],
+                        out=turned[:, cols], lhsT=both[:, 0, cols], rhs=ident[:],
                         is_transpose=True, start=True, stop=False,
                     )
                     nc.tensor.matmul(
-                        out=turned[:, cols], lhsT=with_sin[:, cols], rhs=swap[:],
+                        out=turned[:, cols], lhsT=both[:, 1, cols], rhs=swap[:],
                         is_transpose=True, start=False, stop=True,
                     )
+                else:
+                    nc.tensor.transpose(out=turned[:, cols], in_=both[:, 0, cols], identity=ident[:])
 
         def copy_out(h):
             pair, i = divmod(h, PAIR)
@@ -275,10 +282,10 @@ def tile_qwencausalselfattention_pa_kernel(
             first_head = pair * PAIR
             if first_head < Q_HEADS:
                 rows, first_row = result_rows[0], first_head
-            elif first_head < ROTATED_HEADS:
-                rows, first_row = result_rows[1], first_head - Q_HEADS
+            elif first_head < FIRST_K_HEAD:
+                rows, first_row = result_rows[2], first_head - Q_HEADS
             else:
-                rows, first_row = result_rows[2], first_head - ROTATED_HEADS
+                rows, first_row = result_rows[1], first_head - FIRST_K_HEAD
             nc.scalar.dma_start(
                 out=rows[first_row : first_row + PAIR].rearrange("h m c -> m h c"),
                 in_=results[pair][:],

@@ -36,7 +36,7 @@ RUN = 2
 FIRST_CHUNKS = PASSES + 3
 PSUM_BANKS_PER_KIND = 4
 VECTOR_COLS_FIRST = 256
-VECTOR_COLS = 128
+GPSIMD_COLS = 224
 
 FLOPS = 2 * TOKENS * DIM * HEADS * HEAD_DIM
 
@@ -194,11 +194,24 @@ def tile_qwencausalselfattention_pa_kernel(
         def regroup(n):
             grouped = grouped_pool.tile([P, BLOCK_COLS, PACK], BF16, align_bytes=64, name="grouped")
             w_grouped[n] = grouped
-            vector_cols = VECTOR_COLS_FIRST if n < FIRST_CHUNKS else VECTOR_COLS
-            for copy, cols in (
-                (nc.vector.tensor_copy, slice(0, vector_cols)),
-                (nc.scalar.copy, slice(vector_cols, BLOCK_COLS)),
-            ):
+            if n < FIRST_CHUNKS:
+                first_cols = VECTOR_COLS_FIRST
+                shares = (
+                    (nc.vector.tensor_copy, slice(0, first_cols)),
+                    (nc.scalar.copy, slice(first_cols, BLOCK_COLS)),
+                )
+            else:
+                first_cols = GPSIMD_COLS
+                shares = ((nc.scalar.copy, slice(first_cols, BLOCK_COLS)),)
+                nc.gpsimd.tensor_scalar(
+                    out=grouped[:, 0:first_cols, :],
+                    in0=w_raw[n][:, :, 0:first_cols].rearrange("p j c -> p c j"),
+                    scalar1=1.0,
+                    scalar2=0.0,
+                    op0=MULT,
+                    op1=ADD,
+                )
+            for copy, cols in shares:
                 copy(
                     out=grouped[:, cols, :].rearrange("p (c i) j -> p c j i", i=4),
                     in_=w_raw[n][:, :, cols].rearrange("p j (c i) -> p c j i", i=4),

@@ -37,6 +37,7 @@ FIRST_CHUNKS = PASSES + 3
 PSUM_BANKS_PER_KIND = 4
 VECTOR_COLS_FIRST = 256
 GPSIMD_COLS = 224
+KV_COLS = V_HEADS * HEAD_DIM
 
 FLOPS = 2 * TOKENS * DIM * HEADS * HEAD_DIM
 
@@ -53,7 +54,7 @@ def tile_qwencausalselfattention_pa_kernel(
         grouped_pool = stack.enter_context(tc.tile_pool(name="grouped_pool", bufs=4))
         codes_pool = stack.enter_context(tc.tile_pool(name="codes_pool", bufs=3))
         product_pool = stack.enter_context(tc.tile_pool(name="product_pool", bufs=4))
-        result_pool = stack.enter_context(tc.tile_pool(name="result_pool", bufs=3))
+        result_pool = stack.enter_context(tc.tile_pool(name="result_pool", bufs=HEADS // PAIR))
         psum = stack.enter_context(tc.psum_pool(name="psum", bufs=PSUM_BANKS_PER_KIND))
         stack.enter_context(tc.manual_schedule())
 
@@ -100,16 +101,23 @@ def tile_qwencausalselfattention_pa_kernel(
                     ),
                 )
             else:
-                v_cols = V_HEADS * HEAD_DIM
-                nc.sync.dma_start(
-                    out=raw[:, :, 0:v_cols],
-                    in_=wv_k[k_rows, :].rearrange("(p j) c -> p j c", j=PACK),
-                )
-                nc.sync.dma_start(
-                    out=raw[:, :, v_cols:BLOCK_COLS],
-                    in_=wk_k[k_rows, :].rearrange("(p j) c -> p j c", j=PACK),
-                )
+                flat = raw[:].rearrange("p j c -> p (j c)")
+                for half, w in enumerate((wv_k, wk_k)):
+                    nc.sync.dma_start(
+                        out=flat[:, half * PACK * KV_COLS : (half + 1) * PACK * KV_COLS],
+                        in_=w[k_rows, :].rearrange("(p j) c -> p (j c)", j=PACK),
+                    )
             w_raw.append(raw)
+
+        def raw_columns(n, cols):
+            if n // PASSES * BLOCK_HEADS < Q_HEADS:
+                return w_raw[n][:, :, cols]
+            half = cols.start // KV_COLS
+            assert cols.stop <= (half + 1) * KV_COLS
+            halves = w_raw[n][:].rearrange("p j c -> p (j c)").rearrange(
+                "p (s j c) -> p s j c", s=2, j=PACK
+            )
+            return halves[:, half, :, cols.start - half * KV_COLS : cols.stop - half * KV_COLS]
 
         ident = const.tile([P, P], F32)
         make_identity(nc, ident[:])
@@ -201,11 +209,11 @@ def tile_qwencausalselfattention_pa_kernel(
                     (nc.scalar.copy, slice(first_cols, BLOCK_COLS)),
                 )
             else:
-                first_cols = GPSIMD_COLS
+                first_cols = GPSIMD_COLS if n // PASSES * BLOCK_HEADS < Q_HEADS else KV_COLS
                 shares = ((nc.scalar.copy, slice(first_cols, BLOCK_COLS)),)
                 nc.gpsimd.tensor_scalar(
                     out=grouped[:, 0:first_cols, :],
-                    in0=w_raw[n][:, :, 0:first_cols].rearrange("p j c -> p c j"),
+                    in0=raw_columns(n, slice(0, first_cols)).rearrange("p j c -> p c j"),
                     scalar1=1.0,
                     scalar2=0.0,
                     op0=MULT,
@@ -214,7 +222,7 @@ def tile_qwencausalselfattention_pa_kernel(
             for copy, cols in shares:
                 copy(
                     out=grouped[:, cols, :].rearrange("p (c i) j -> p c j i", i=4),
-                    in_=w_raw[n][:, :, cols].rearrange("p j (c i) -> p c j i", i=4),
+                    in_=raw_columns(n, cols).rearrange("p j (c i) -> p c j i", i=4),
                 )
 
         def quantise(n):
@@ -299,7 +307,7 @@ def tile_qwencausalselfattention_pa_kernel(
                 rows, first_row = result_rows[2], first_head - Q_HEADS
             else:
                 rows, first_row = result_rows[1], first_head - FIRST_K_HEAD
-            nc.scalar.dma_start(
+            nc.sync.dma_start(
                 out=rows[first_row : first_row + PAIR].rearrange("h m c -> m h c"),
                 in_=results[pair][:],
             )

@@ -36,7 +36,7 @@ RUN = 2
 FIRST_CHUNKS = PASSES + 3
 PSUM_BANKS_PER_KIND = 4
 VECTOR_COLS_FIRST = 256
-GPSIMD_COLS = 224
+GPSIMD_COLS = 272
 KV_COLS = V_HEADS * HEAD_DIM
 
 FLOPS = 2 * TOKENS * DIM * HEADS * HEAD_DIM

@@ -30,11 +30,12 @@ BLOCK_HEADS = 4
 BLOCK_COLS = BLOCK_HEADS * HEAD_DIM
 BLOCKS = HEADS // BLOCK_HEADS
 CHUNKS = BLOCKS * PASSES
-CHUNKS_PER_HEAD = PASSES // BLOCK_HEADS
 PAIR = 2
-RUN = 2
-FIRST_CHUNKS = PASSES + 3
-PSUM_BANKS_PER_KIND = 4
+RUN_PASSES = 2
+STEPS_PER_BLOCK = PASSES // RUN_PASSES
+STEPS_WITH_PASSES = (BLOCKS - 1) * STEPS_PER_BLOCK
+GROUP_BANKS = 4
+VECTOR_CHUNKS = PASSES + 1
 VECTOR_COLS_FIRST = 256
 GPSIMD_COLS = 272
 KV_COLS = V_HEADS * HEAD_DIM
@@ -53,9 +54,9 @@ def tile_qwencausalselfattention_pa_kernel(
         raw_pool = stack.enter_context(tc.tile_pool(name="raw_pool", bufs=CHUNKS))
         grouped_pool = stack.enter_context(tc.tile_pool(name="grouped_pool", bufs=4))
         codes_pool = stack.enter_context(tc.tile_pool(name="codes_pool", bufs=3))
-        product_pool = stack.enter_context(tc.tile_pool(name="product_pool", bufs=4))
-        result_pool = stack.enter_context(tc.tile_pool(name="result_pool", bufs=HEADS // PAIR))
-        psum = stack.enter_context(tc.psum_pool(name="psum", bufs=PSUM_BANKS_PER_KIND))
+        product_pool = stack.enter_context(tc.tile_pool(name="product_pool", bufs=6))
+        result_pool = stack.enter_context(tc.tile_pool(name="result_pool", bufs=6))
+        psum = stack.enter_context(tc.psum_pool(name="psum", bufs=GROUP_BANKS))
         stack.enter_context(tc.manual_schedule())
 
         x_rows = x.flatten_outer_dims().rearrange("(m f) k -> m f k", f=TOKENS_PER_PARTITION)
@@ -119,6 +120,9 @@ def tile_qwencausalselfattention_pa_kernel(
             )
             return halves[:, half, :, cols.start - half * KV_COLS : cols.stop - half * KV_COLS]
 
+        def group(block):
+            return "group%d" % (block % 2)
+
         ident = const.tile([P, P], F32)
         make_identity(nc, ident[:])
         swap = const.tile([P, P], F32)
@@ -136,13 +140,13 @@ def tile_qwencausalselfattention_pa_kernel(
         nc.vector.tensor_copy(out=bias_f32[:], in_=bias_rows[:])
         tables = const.tile([P, 2, TOKENS], F32)
         for i, rows in enumerate((cos_f32, sin_f32)):
-            turned = psum.tile([P, TOKENS], F32, tag="turned")
+            turned = psum.tile([P, TOKENS], F32, tag=group(1))
             for f in range(TOKENS_PER_PARTITION):
                 nc.tensor.transpose(
                     out=turned[:, f * P : (f + 1) * P], in_=rows[:, f, :], identity=ident[:]
                 )
             nc.scalar.copy(out=tables[:, i, :], in_=turned[:])
-        turned = psum.tile([P, TOKENS], F32, tag="turned")
+        turned = psum.tile([P, TOKENS], F32, tag=group(1))
         nc.tensor.transpose(out=turned[:, 0:P], in_=bias_f32[:], identity=ident[:])
         bias_t = const.tile([P, HEADS], F32)
         nc.scalar.copy(out=bias_t[:], in_=turned[:, 0:HEADS])
@@ -158,7 +162,7 @@ def tile_qwencausalselfattention_pa_kernel(
                 grouped = x_pool.tile([P, TOKENS * PACK], BF16, align_bytes=64, name="x_grouped")
                 x_grouped.append(grouped)
                 for half in range(2):
-                    turned = psum.tile([P, TOKENS], F32, tag="turned")
+                    turned = psum.tile([P, TOKENS], F32, tag=group(1))
                     for u in range(2):
                         for f in range(2 * half, 2 * half + 2):
                             column = u * half_tokens + (f - 2 * half) * P
@@ -202,7 +206,7 @@ def tile_qwencausalselfattention_pa_kernel(
         def regroup(n):
             grouped = grouped_pool.tile([P, BLOCK_COLS, PACK], BF16, align_bytes=64, name="grouped")
             w_grouped[n] = grouped
-            if n < FIRST_CHUNKS:
+            if n < VECTOR_CHUNKS:
                 first_cols = VECTOR_COLS_FIRST
                 shares = (
                     (nc.vector.tensor_copy, slice(0, first_cols)),
@@ -241,9 +245,9 @@ def tile_qwencausalselfattention_pa_kernel(
             )
 
         def multiply(h, g):
-            if g == 0:
-                products[h] = psum.tile([P, TOKENS], F32, tag="product", name="product")
             b, i = divmod(h, BLOCK_HEADS)
+            if g == 0:
+                products[h] = psum.tile([P, TOKENS], F32, tag=group(b), name="product")
             cols = slice(i * HEAD_DIM, (i + 1) * HEAD_DIM)
             nc.tensor.matmul_mx(
                 out=products[h][:],
@@ -275,7 +279,7 @@ def tile_qwencausalselfattention_pa_kernel(
 
         def turn_back(h):
             both = factors[h]
-            turned = psum.tile([P, TOKENS], F32, tag="turned", name="turned")
+            turned = psum.tile([P, TOKENS], F32, tag=group(h // BLOCK_HEADS), name="turned")
             turned_banks[h] = turned
             for f in range(TOKENS_PER_PARTITION):
                 cols = slice(f * P, (f + 1) * P)
@@ -291,13 +295,13 @@ def tile_qwencausalselfattention_pa_kernel(
                 else:
                     nc.tensor.transpose(out=turned[:, cols], in_=both[:, 0, cols], identity=ident[:])
 
-        def copy_out(h):
+        def copy_out(h, copy):
             pair, i = divmod(h, PAIR)
             if i == 0:
                 results[pair] = result_pool.tile(
                     [P, PAIR, TOKENS_PER_PARTITION * HEAD_DIM], F32, name="result"
                 )
-            nc.scalar.copy(out=results[pair][:, i, :], in_=turned_banks[h][:])
+            copy(out=results[pair][:, i, :], in_=turned_banks[h][:])
 
         def store(pair):
             first_head = pair * PAIR
@@ -312,34 +316,53 @@ def tile_qwencausalselfattention_pa_kernel(
                 in_=results[pair][:],
             )
 
-        def prepare(n):
-            if n < CHUNKS:
-                regroup(n)
-            if 0 < n <= CHUNKS:
-                quantise(n - 1)
+        progress = {"regrouped": 0, "quantised": 0}
 
-        for n in range(FIRST_CHUNKS):
-            prepare(n)
-            if 0 < n <= PASSES:
-                for h in range(BLOCK_HEADS):
-                    multiply(h, n - 1)
+        def prepare_up_to(last):
+            while progress["quantised"] <= min(last, CHUNKS - 1):
+                n = progress["quantised"]
+                ahead = n + 1 if n + 1 < VECTOR_CHUNKS else n
+                while progress["regrouped"] <= ahead:
+                    regroup(progress["regrouped"])
+                    progress["regrouped"] += 1
+                quantise(n)
+                progress["quantised"] += 1
 
-        next_chunk = FIRST_CHUNKS
-        for first_head in range(0, HEADS, RUN):
-            heads = range(first_head, first_head + RUN)
-            for h in heads:
-                if BLOCK_HEADS <= h + RUN < HEADS:
-                    for g in range(PASSES):
-                        multiply(h + RUN, g)
+        def run_of_passes(step):
+            block, part = divmod(step, STEPS_PER_BLOCK)
+            for g in range(part * RUN_PASSES, (part + 1) * RUN_PASSES):
+                for h in range((block + 1) * BLOCK_HEADS, (block + 2) * BLOCK_HEADS):
+                    multiply(h, g)
+
+        def last_chunk_of(step):
+            return PASSES + (step + 1) * RUN_PASSES - 1
+
+        for g in range(PASSES):
+            prepare_up_to(g)
+            for h in range(BLOCK_HEADS):
+                multiply(h, g)
+        prepare_up_to(last_chunk_of(0))
+
+        for step in range(STEPS_WITH_PASSES - 1):
+            heads = range(step * PAIR, (step + 1) * PAIR)
+            run_of_passes(step)
             for h in heads:
                 add_bias_and_scale(h)
             for h in heads:
                 turn_back(h)
-            for n in range(next_chunk, next_chunk + RUN * CHUNKS_PER_HEAD):
-                prepare(n)
-                if n == next_chunk and first_head > 0 and first_head % PAIR == 0:
-                    store(first_head // PAIR - 1)
-            next_chunk += RUN * CHUNKS_PER_HEAD
+            prepare_up_to(last_chunk_of(step + 1))
             for h in heads:
-                copy_out(h)
-        store(HEADS // PAIR - 1)
+                copy_out(h, nc.scalar.copy)
+            store(step)
+
+        run_of_passes(STEPS_WITH_PASSES - 1)
+        heads = range((STEPS_WITH_PASSES - 1) * PAIR, HEADS)
+        for h in heads:
+            add_bias_and_scale(h)
+        for h in heads:
+            turn_back(h)
+        for h in heads:
+            by_vector = h % PAIR == 1 and h >= HEADS - 2 * PAIR
+            copy_out(h, nc.vector.tensor_copy if by_vector else nc.scalar.copy)
+            if h % PAIR == 1:
+                store(h // PAIR)

@@ -303,17 +303,17 @@ def tile_qwencausalselfattention_pa_kernel(
                 )
             copy(out=results[pair][:, i, :], in_=turned_banks[h][:])
 
-        def store(pair):
-            first_head = pair * PAIR
+        def store(first_head, heads):
             if first_head < Q_HEADS:
                 rows, first_row = result_rows[0], first_head
             elif first_head < FIRST_K_HEAD:
                 rows, first_row = result_rows[2], first_head - Q_HEADS
             else:
                 rows, first_row = result_rows[1], first_head - FIRST_K_HEAD
+            pair, i = divmod(first_head, PAIR)
             nc.sync.dma_start(
-                out=rows[first_row : first_row + PAIR].rearrange("h m c -> m h c"),
-                in_=results[pair][:],
+                out=rows[first_row : first_row + heads].rearrange("h m c -> m h c"),
+                in_=results[pair][:, i : i + heads, :],
             )
 
         progress = {"regrouped": 0, "quantised": 0}
@@ -330,9 +330,11 @@ def tile_qwencausalselfattention_pa_kernel(
 
         def run_of_passes(step):
             block, part = divmod(step, STEPS_PER_BLOCK)
-            for g in range(part * RUN_PASSES, (part + 1) * RUN_PASSES):
-                for h in range((block + 1) * BLOCK_HEADS, (block + 2) * BLOCK_HEADS):
-                    multiply(h, g)
+            first_head = (block + 1) * BLOCK_HEADS
+            for pair_head in range(first_head, first_head + BLOCK_HEADS, PAIR):
+                for g in range(part * RUN_PASSES, (part + 1) * RUN_PASSES):
+                    for h in range(pair_head, pair_head + PAIR):
+                        multiply(h, g)
 
         def last_chunk_of(step):
             return PASSES + (step + 1) * RUN_PASSES - 1
@@ -353,7 +355,7 @@ def tile_qwencausalselfattention_pa_kernel(
             prepare_up_to(last_chunk_of(step + 1))
             for h in heads:
                 copy_out(h, nc.scalar.copy)
-            store(step)
+            store(step * PAIR, PAIR)
 
         run_of_passes(STEPS_WITH_PASSES - 1)
         heads = range((STEPS_WITH_PASSES - 1) * PAIR, HEADS)
@@ -364,5 +366,7 @@ def tile_qwencausalselfattention_pa_kernel(
         for h in heads:
             by_vector = h % PAIR == 1 and h >= HEADS - 2 * PAIR
             copy_out(h, nc.vector.tensor_copy if by_vector else nc.scalar.copy)
-            if h % PAIR == 1:
-                store(h // PAIR)
+            if h >= HEADS - PAIR:
+                store(h, 1)
+            elif h % PAIR == 1:
+                store(h - 1, PAIR)

@@ -173,7 +173,7 @@ def tile_qwencausalselfattention_pa_kernel(
                                 ],
                                 identity=ident[:],
                             )
-                    copy = nc.vector.tensor_copy if half == 0 else nc.scalar.copy
+                    copy = nc.scalar.copy
                     copy(
                         out=grouped[:]
                         .bitcast(F32)[:, half * TOKENS : (half + 1) * TOKENS]

@@ -138,19 +138,6 @@ def tile_qwencausalselfattention_pa_kernel(
         )
         bias_f32 = setup.tile([P, HEAD_DIM], F32)
         nc.vector.tensor_copy(out=bias_f32[:], in_=bias_rows[:])
-        tables = const.tile([P, 2, TOKENS], F32)
-        for i, rows in enumerate((cos_f32, sin_f32)):
-            turned = psum.tile([P, TOKENS], F32, tag=group(1))
-            for f in range(TOKENS_PER_PARTITION):
-                nc.tensor.transpose(
-                    out=turned[:, f * P : (f + 1) * P], in_=rows[:, f, :], identity=ident[:]
-                )
-            nc.scalar.copy(out=tables[:, i, :], in_=turned[:])
-        turned = psum.tile([P, TOKENS], F32, tag=group(1))
-        nc.tensor.transpose(out=turned[:, 0:P], in_=bias_f32[:], identity=ident[:])
-        bias_t = const.tile([P, HEADS], F32)
-        nc.scalar.copy(out=bias_t[:], in_=turned[:, 0:HEADS])
-
         x_codes = const.tile([P, PASSES, TOKENS], U32, align_bytes=64)
         x_scales = const.tile([P, PASSES, TOKENS], U8, align_bytes=64)
         words_per_token = K_PASS // 2
@@ -186,6 +173,19 @@ def tile_qwencausalselfattention_pa_kernel(
                     scales=x_scales[:, g - 1, :],
                     in_=x_grouped[g - 1][:],
                 )
+
+        tables = const.tile([P, 2, TOKENS], F32)
+        for i, rows in enumerate((cos_f32, sin_f32)):
+            turned = psum.tile([P, TOKENS], F32, tag=group(1))
+            for f in range(TOKENS_PER_PARTITION):
+                nc.tensor.transpose(
+                    out=turned[:, f * P : (f + 1) * P], in_=rows[:, f, :], identity=ident[:]
+                )
+            nc.scalar.copy(out=tables[:, i, :], in_=turned[:])
+        turned = psum.tile([P, TOKENS], F32, tag=group(1))
+        nc.tensor.transpose(out=turned[:, 0:P], in_=bias_f32[:], identity=ident[:])
+        bias_t = const.tile([P, HEADS], F32)
+        nc.scalar.copy(out=bias_t[:], in_=turned[:, 0:HEADS])
 
         result_rows = [
             out.rearrange("b h (m f) d -> (b h) m (f d)", f=TOKENS_PER_PARTITION)

@@ -366,7 +366,4 @@ def tile_qwencausalselfattention_pa_kernel(
         for h in heads:
             by_vector = h % PAIR == 1 and h >= HEADS - 2 * PAIR
             copy_out(h, nc.vector.tensor_copy if by_vector else nc.scalar.copy)
-            if h >= HEADS - PAIR:
-                store(h, 1)
-            elif h % PAIR == 1:
-                store(h - 1, PAIR)
+            store(h, 1)

@@ -358,12 +358,14 @@ def tile_qwencausalselfattention_pa_kernel(
             store(step * PAIR, PAIR)
 
         run_of_passes(STEPS_WITH_PASSES - 1)
-        heads = range((STEPS_WITH_PASSES - 1) * PAIR, HEADS)
+        first_left = (STEPS_WITH_PASSES - 1) * PAIR
+        heads = [
+            *range(Q_HEADS, FIRST_K_HEAD), *range(first_left, Q_HEADS), *range(FIRST_K_HEAD, HEADS)
+        ]
         for h in heads:
             add_bias_and_scale(h)
         for h in heads:
             turn_back(h)
         for h in heads:
-            by_vector = h % PAIR == 1 and h >= HEADS - 2 * PAIR
-            copy_out(h, nc.vector.tensor_copy if by_vector else nc.scalar.copy)
+            copy_out(h, nc.vector.tensor_copy if h == heads[-1] else nc.scalar.copy)
             store(h, 1)

from contextlib import ExitStack

import concourse.mybir as mybir
from concourse.masks import make_identity

F32 = mybir.dt.float32
BF16 = mybir.dt.bfloat16
U32 = mybir.dt.uint32
U8 = mybir.dt.uint8
FP8X4 = mybir.dt.float8_e4m3fn_x4
ADD = mybir.AluOpType.add
MULT = mybir.AluOpType.mult
IDENTITY = mybir.ActivationFunctionType.Identity

P = 128
PACK = 4
K_PASS = P * PACK
TOKENS = 512
DIM = 2048
PASSES = DIM // K_PASS
TOKENS_PER_PARTITION = TOKENS // P
HEAD_DIM = 128
HALF = HEAD_DIM // 2
Q_HEADS = 16
V_HEADS = 2
K_HEADS = 2
FIRST_K_HEAD = Q_HEADS + V_HEADS
HEADS = FIRST_K_HEAD + K_HEADS
BLOCK_HEADS = 4
BLOCK_COLS = BLOCK_HEADS * HEAD_DIM
BLOCKS = HEADS // BLOCK_HEADS
CHUNKS = BLOCKS * PASSES
PAIR = 2
RUN_PASSES = 2
STEPS_PER_BLOCK = PASSES // RUN_PASSES
STEPS_WITH_PASSES = (BLOCKS - 1) * STEPS_PER_BLOCK
GROUP_BANKS = 4
VECTOR_CHUNKS = PASSES + 1
VECTOR_COLS_FIRST = 256
GPSIMD_COLS = 272
KV_COLS = V_HEADS * HEAD_DIM

FLOPS = 2 * TOKENS * DIM * HEADS * HEAD_DIM


def tile_qwencausalselfattention_pa_kernel(
    tc, x, cos, sin, wq_k, wq_b, wk_k, wk_b, wv_k, wv_b, out_0, out_1, out_2
):
    nc = tc.nc
    with ExitStack() as stack:
        const = stack.enter_context(tc.tile_pool(name="const", bufs=1))
        setup = stack.enter_context(tc.tile_pool(name="setup", bufs=1))
        x_pool = stack.enter_context(tc.tile_pool(name="x_pool", bufs=PASSES))
        raw_pool = stack.enter_context(tc.tile_pool(name="raw_pool", bufs=CHUNKS))
        grouped_pool = stack.enter_context(tc.tile_pool(name="grouped_pool", bufs=4))
        codes_pool = stack.enter_context(tc.tile_pool(name="codes_pool", bufs=3))
        product_pool = stack.enter_context(tc.tile_pool(name="product_pool", bufs=6))
        result_pool = stack.enter_context(tc.tile_pool(name="result_pool", bufs=6))
        psum = stack.enter_context(tc.psum_pool(name="psum", bufs=GROUP_BANKS))
        stack.enter_context(tc.manual_schedule())

        x_rows = x.flatten_outer_dims().rearrange("(m f) k -> m f k", f=TOKENS_PER_PARTITION)
        x_raw = []
        for g in range(PASSES):
            x_slice = x_pool.tile([P, TOKENS_PER_PARTITION * K_PASS], BF16, name="x_slice")
            nc.sync.dma_start(
                out=x_slice[:].rearrange("m (f k) -> m f k", f=TOKENS_PER_PARTITION),
                in_=x_rows[:, :, g * K_PASS : (g + 1) * K_PASS],
            )
            x_raw.append(x_slice)

        cos_raw = setup.tile([P, TOKENS_PER_PARTITION, HEAD_DIM], BF16)
        sin_raw = setup.tile([P, TOKENS_PER_PARTITION, HEAD_DIM], BF16)
        nc.scalar.dma_start(
            out=cos_raw[:], in_=cos.rearrange("(m f) d -> m f d", f=TOKENS_PER_PARTITION)
        )
        nc.scalar.dma_start(
            out=sin_raw[:], in_=sin.rearrange("(m f) d -> m f d", f=TOKENS_PER_PARTITION)
        )
        bias_rows = setup.tile([P, HEAD_DIM], BF16)
        nc.vector.memset(bias_rows[:], 0.0)
        nc.scalar.dma_start(
            out=bias_rows[0:Q_HEADS, :], in_=wq_b.rearrange("(h d) -> h d", d=HEAD_DIM)
        )
        nc.scalar.dma_start(
            out=bias_rows[Q_HEADS:FIRST_K_HEAD, :], in_=wv_b.rearrange("(h d) -> h d", d=HEAD_DIM)
        )
        nc.scalar.dma_start(
            out=bias_rows[FIRST_K_HEAD:HEADS, :], in_=wk_b.rearrange("(h d) -> h d", d=HEAD_DIM)
        )

        w_raw = []
        for n in range(CHUNKS):
            b, g = divmod(n, PASSES)
            k_rows = slice(g * K_PASS, (g + 1) * K_PASS)
            raw = raw_pool.tile([P, PACK, BLOCK_COLS], BF16, name="raw")
            if b * BLOCK_HEADS < Q_HEADS:
                nc.sync.dma_start(
                    out=raw[:],
                    in_=wq_k[k_rows, b * BLOCK_COLS : (b + 1) * BLOCK_COLS].rearrange(
                        "(p j) c -> p j c", j=PACK
                    ),
                )
            else:
                flat = raw[:].rearrange("p j c -> p (j c)")
                for half, w in enumerate((wv_k, wk_k)):
                    nc.sync.dma_start(
                        out=flat[:, half * PACK * KV_COLS : (half + 1) * PACK * KV_COLS],
                        in_=w[k_rows, :].rearrange("(p j) c -> p (j c)", j=PACK),
                    )
            w_raw.append(raw)

        def raw_columns(n, cols):
            if n // PASSES * BLOCK_HEADS < Q_HEADS:
                return w_raw[n][:, :, cols]
            half = cols.start // KV_COLS
            assert cols.stop <= (half + 1) * KV_COLS
            halves = w_raw[n][:].rearrange("p j c -> p (j c)").rearrange(
                "p (s j c) -> p s j c", s=2, j=PACK
            )
            return halves[:, half, :, cols.start - half * KV_COLS : cols.stop - half * KV_COLS]

        def group(block):
            return "group%d" % (block % 2)

        ident = const.tile([P, P], F32)
        make_identity(nc, ident[:])
        swap = const.tile([P, P], F32)
        nc.vector.tensor_copy(out=swap[:, 0:HALF], in_=ident[:, HALF:P])
        nc.vector.tensor_copy(out=swap[:, HALF:P], in_=ident[:, 0:HALF])

        cos_f32 = setup.tile([P, TOKENS_PER_PARTITION, HEAD_DIM], F32)
        sin_f32 = setup.tile([P, TOKENS_PER_PARTITION, HEAD_DIM], F32)
        nc.vector.tensor_copy(out=cos_f32[:], in_=cos_raw[:])
        nc.vector.tensor_copy(out=sin_f32[:, :, 0:HALF], in_=sin_raw[:, :, HALF:HEAD_DIM])
        nc.vector.tensor_scalar_mul(
            out=sin_f32[:, :, HALF:HEAD_DIM], in0=sin_raw[:, :, 0:HALF], scalar1=-1.0
        )
        bias_f32 = setup.tile([P, HEAD_DIM], F32)
        nc.vector.tensor_copy(out=bias_f32[:], in_=bias_rows[:])
        x_codes = const.tile([P, PASSES, TOKENS], U32, align_bytes=64)
        x_scales = const.tile([P, PASSES, TOKENS], U8, align_bytes=64)
        words_per_token = K_PASS // 2
        half_tokens = TOKENS // 2
        x_grouped = []
        for g in range(PASSES + 1):
            if g < PASSES:
                x_words = x_raw[g][:].bitcast(F32)
                grouped = x_pool.tile([P, TOKENS * PACK], BF16, align_bytes=64, name="x_grouped")
                x_grouped.append(grouped)
                for half in range(2):
                    turned = psum.tile([P, TOKENS], F32, tag=group(1))
                    for u in range(2):
                        for f in range(2 * half, 2 * half + 2):
                            column = u * half_tokens + (f - 2 * half) * P
                            nc.tensor.transpose(
                                out=turned[:, column : column + P],
                                in_=x_words[
                                    :, f * words_per_token + u : (f + 1) * words_per_token : 2
                                ],
                                identity=ident[:],
                            )
                    copy = nc.scalar.copy
                    copy(
                        out=grouped[:]
                        .bitcast(F32)[:, half * TOKENS : (half + 1) * TOKENS]
                        .rearrange("p (n u) -> p n u", u=2),
                        in_=turned[:].rearrange("p (u n) -> p n u", u=2),
                    )
            if g > 0:
                nc.vector.quantize_mx(
                    out=x_codes[:, g - 1, :].bitcast(FP8X4),
                    scales=x_scales[:, g - 1, :],
                    in_=x_grouped[g - 1][:],
                )

        tables = const.tile([P, 2, TOKENS], F32)
        for i, rows in enumerate((cos_f32, sin_f32)):
            turned = psum.tile([P, TOKENS], F32, tag=group(1))
            for f in range(TOKENS_PER_PARTITION):
                nc.tensor.transpose(
                    out=turned[:, f * P : (f + 1) * P], in_=rows[:, f, :], identity=ident[:]
                )
            nc.scalar.copy(out=tables[:, i, :], in_=turned[:])
        turned = psum.tile([P, TOKENS], F32, tag=group(1))
        nc.tensor.transpose(out=turned[:, 0:P], in_=bias_f32[:], identity=ident[:])
        bias_t = const.tile([P, HEADS], F32)
        nc.scalar.copy(out=bias_t[:], in_=turned[:, 0:HEADS])

        result_rows = [
            out.rearrange("b h (m f) d -> (b h) m (f d)", f=TOKENS_PER_PARTITION)
            for out in (out_0, out_1, out_2)
        ]

        w_grouped = {}
        w_codes = {}
        w_scales = {}
        products = {}
        factors = {}
        turned_banks = {}
        results = {}

        def rotated(h):
            return h < Q_HEADS or h >= FIRST_K_HEAD

        def regroup(n):
            grouped = grouped_pool.tile([P, BLOCK_COLS, PACK], BF16, align_bytes=64, name="grouped")
            w_grouped[n] = grouped
            if n < VECTOR_CHUNKS:
                first_cols = VECTOR_COLS_FIRST
                shares = (
                    (nc.vector.tensor_copy, slice(0, first_cols)),
                    (nc.scalar.copy, slice(first_cols, BLOCK_COLS)),
                )
            else:
                first_cols = GPSIMD_COLS if n // PASSES * BLOCK_HEADS < Q_HEADS else KV_COLS
                shares = ((nc.scalar.copy, slice(first_cols, BLOCK_COLS)),)
                nc.gpsimd.tensor_scalar(
                    out=grouped[:, 0:first_cols, :],
                    in0=raw_columns(n, slice(0, first_cols)).rearrange("p j c -> p c j"),
                    scalar1=1.0,
                    scalar2=0.0,
                    op0=MULT,
                    op1=ADD,
                )
            for copy, cols in shares:
                copy(
                    out=grouped[:, cols, :].rearrange("p (c i) j -> p c j i", i=4),
                    in_=raw_columns(n, cols).rearrange("p j (c i) -> p c j i", i=4),
                )

        def quantise(n):
            b, g = divmod(n, PASSES)
            if g == 0:
                w_codes[b] = codes_pool.tile(
                    [P, PASSES, BLOCK_COLS], U32, align_bytes=64, name="w_codes"
                )
                w_scales[b] = codes_pool.tile(
                    [P, PASSES, BLOCK_COLS], U8, align_bytes=64, name="w_scales"
                )
            nc.vector.quantize_mx(
                out=w_codes[b][:, g, :].bitcast(FP8X4),
                scales=w_scales[b][:, g, :],
                in_=w_grouped[n][:].rearrange("p c j -> p (c j)"),
            )

        def multiply(h, g):
            b, i = divmod(h, BLOCK_HEADS)
            if g == 0:
                products[h] = psum.tile([P, TOKENS], F32, tag=group(b), name="product")
            cols = slice(i * HEAD_DIM, (i + 1) * HEAD_DIM)
            nc.tensor.matmul_mx(
                out=products[h][:],
                lhsT=w_codes[b][:, g, cols].bitcast(FP8X4),
                lhsT_scale=w_scales[b][:, g, cols],
                rhs=x_codes[:, g, :].bitcast(FP8X4),
                rhs_scale=x_scales[:, g, :],
                start=(g == 0),
                stop=(g == PASSES - 1),
            )

        def add_bias_and_scale(h):
            bias = bias_t[:, h : h + 1]
            both = product_pool.tile([P, 2, TOKENS], F32, name="both")
            factors[h] = both
            if rotated(h):
                nc.vector.scalar_tensor_tensor(
                    out=both[:],
                    in0=products[h][:].unsqueeze(1).to_broadcast([P, 2, TOKENS]),
                    scalar=bias,
                    in1=tables[:],
                    op0=ADD,
                    op1=MULT,
                )
            else:
                nc.scalar.activation(
                    out=both[:, 0, :], in_=products[h][:], func=IDENTITY, bias=bias, scale=1.0
                )

        def turn_back(h):
            both = factors[h]
            turned = psum.tile([P, TOKENS], F32, tag=group(h // BLOCK_HEADS), name="turned")
            turned_banks[h] = turned
            for f in range(TOKENS_PER_PARTITION):
                cols = slice(f * P, (f + 1) * P)
                if rotated(h):
                    nc.tensor.matmul(
                        out=turned[:, cols], lhsT=both[:, 0, cols], rhs=ident[:],
                        is_transpose=True, start=True, stop=False,
                    )
                    nc.tensor.matmul(
                        out=turned[:, cols], lhsT=both[:, 1, cols], rhs=swap[:],
                        is_transpose=True, start=False, stop=True,
                    )
                else:
                    nc.tensor.transpose(out=turned[:, cols], in_=both[:, 0, cols], identity=ident[:])

        def copy_out(h, copy):
            pair, i = divmod(h, PAIR)
            if i == 0:
                results[pair] = result_pool.tile(
                    [P, PAIR, TOKENS_PER_PARTITION * HEAD_DIM], F32, name="result"
                )
            copy(out=results[pair][:, i, :], in_=turned_banks[h][:])

        def store(first_head, heads):
            if first_head < Q_HEADS:
                rows, first_row = result_rows[0], first_head
            elif first_head < FIRST_K_HEAD:
                rows, first_row = result_rows[2], first_head - Q_HEADS
            else:
                rows, first_row = result_rows[1], first_head - FIRST_K_HEAD
            pair, i = divmod(first_head, PAIR)
            nc.sync.dma_start(
                out=rows[first_row : first_row + heads].rearrange("h m c -> m h c"),
                in_=results[pair][:, i : i + heads, :],
            )

        progress = {"regrouped": 0, "quantised": 0}

        def prepare_up_to(last):
            while progress["quantised"] <= min(last, CHUNKS - 1):
                n = progress["quantised"]
                ahead = n + 1 if n + 1 < VECTOR_CHUNKS else n
                while progress["regrouped"] <= ahead:
                    regroup(progress["regrouped"])
                    progress["regrouped"] += 1
                quantise(n)
                progress["quantised"] += 1

        def run_of_passes(step):
            block, part = divmod(step, STEPS_PER_BLOCK)
            first_head = (block + 1) * BLOCK_HEADS
            for pair_head in range(first_head, first_head + BLOCK_HEADS, PAIR):
                for g in range(part * RUN_PASSES, (part + 1) * RUN_PASSES):
                    for h in range(pair_head, pair_head + PAIR):
                        multiply(h, g)

        def last_chunk_of(step):
            return PASSES + (step + 1) * RUN_PASSES - 1

        for g in range(PASSES):
            prepare_up_to(g)
            for h in range(BLOCK_HEADS):
                multiply(h, g)
        prepare_up_to(last_chunk_of(0))

        for step in range(STEPS_WITH_PASSES - 1):
            heads = range(step * PAIR, (step + 1) * PAIR)
            run_of_passes(step)
            for h in heads:
                add_bias_and_scale(h)
            for h in heads:
                turn_back(h)
            prepare_up_to(last_chunk_of(step + 1))
            for h in heads:
                copy_out(h, nc.scalar.copy)
            store(step * PAIR, PAIR)

        run_of_passes(STEPS_WITH_PASSES - 1)
        first_left = (STEPS_WITH_PASSES - 1) * PAIR
        heads = [
            *range(Q_HEADS, FIRST_K_HEAD), *range(first_left, Q_HEADS), *range(FIRST_K_HEAD, HEADS)
        ]
        for h in heads:
            add_bias_and_scale(h)
        for h in heads:
            turn_back(h)
        for h in heads:
            copy_out(h, nc.vector.tensor_copy if h == heads[-1] else nc.scalar.copy)
            store(h, 1)
